import numpy as np
import ml_dtypes


def mxq(x, axis, fmt="e4m3"):
    dtype, down = {"e4m3": (ml_dtypes.float8_e4m3fn, 7), "e5m2": (ml_dtypes.float8_e5m2, 14)}[fmt]
    v = np.moveaxis(np.asarray(x, np.float32).astype(ml_dtypes.bfloat16).astype(np.float64), axis, -1)
    blocks = v.reshape(v.shape[:-1] + (-1, 32))
    amax = np.abs(blocks).max(-1, keepdims=True)
    byte = np.maximum(np.where(amax > 0, np.frexp(amax)[1] - 1 + 127, 0) - down, 1)
    scale = np.exp2(byte - 127.0)
    codes = (blocks / scale).astype(np.float32).astype(dtype).astype(np.float64)
    return np.moveaxis((codes * scale).reshape(v.shape), -1, axis)


WIDE = False


def mx_kscale(k):
    if not WIDE:
        return np.ones(k)
    levels = np.array([10, -10, 5, -5, 0])
    a = np.random.permutation(np.resize(levels, k // 512 * 4)).reshape(k // 512, 4)
    idx = np.arange(k)
    return np.exp2(a[idx // 512, idx % 128 // 32])


BF16 = ml_dtypes.bfloat16


def bf(x):
    return np.asarray(x, np.float32).astype(BF16)


def f64(x):
    return np.asarray(x).astype(np.float64)


E2M1 = np.array([0.0, 0.5, 1.0, 1.5, 2.0, 3.0, 4.0, 6.0, -0.0, -0.5, -1.0, -1.5, -2.0, -3.0, -4.0, -6.0])


def pack_weight(w, fmt):
    k, n = w.shape
    w = f64(bf(w)).reshape(k // 32, 32, n)
    amax = np.abs(w).max(1)
    if fmt == "e4m3":
        byte = np.frexp(amax)[1] - 1 + 127 - 7
    else:
        mant, ex = np.frexp(amax / 6.0)
        byte = np.where(mant > 0.5, ex, ex - 1) + 127
    byte = np.clip(np.where(amax > 0, byte, 1), 1, 254)
    scaled = (w * np.exp2(127.0 - byte)[:, None, :]).reshape(k, n).astype(np.float32)
    by_word = np.ascontiguousarray(scaled.reshape(k // 512, 128, 4, n).transpose(0, 1, 3, 2))
    if fmt == "e4m3":
        words = by_word.astype(ml_dtypes.float8_e4m3fn).view(np.uint8)
    else:
        c = by_word.astype(ml_dtypes.float4_e2m1fn).view(np.uint8) & 0xF
        words = c[..., 0::2] | (c[..., 1::2] << 4)
    return np.ascontiguousarray(words), np.ascontiguousarray(byte.astype(np.uint8).reshape(k // 512, 16, n))


def unpack_weight(words, scales, fmt):
    g, p, n, _ = words.shape
    if fmt == "e4m3":
        vals = np.ascontiguousarray(words).view(ml_dtypes.float8_e4m3fn).astype(np.float64)
    else:
        nib = np.empty((g, p, n, 4), np.uint8)
        nib[..., 0::2] = words & 0xF
        nib[..., 1::2] = words >> 4
        vals = E2M1[nib]
    vals = vals * np.repeat(np.exp2(scales.astype(np.float64) - 127.0), 8, axis=1)[..., None]
    return vals.transpose(0, 1, 3, 2).reshape(g * 512, n)


B, D_IN, D_OUT = 128, 16384, 1024
EPS = 0.01
FMT = "e4m3"


def setup_inputs():
    s, t = mx_kscale(D_IN), mx_kscale(D_OUT)
    x = bf(np.random.standard_normal((B, D_IN)) * s)
    W = np.random.standard_normal((D_OUT, D_IN)) / np.sqrt(D_IN) / s[None, :] * t[:, None]
    W_words, W_scales = pack_weight(np.ascontiguousarray(W.T), FMT)
    b = bf(np.random.standard_normal(D_OUT) * 0.3 * t)
    g = np.random.standard_normal((D_OUT, D_OUT)) / np.sqrt(D_OUT) / t[None, :]
    g_words, g_scales = pack_weight(np.ascontiguousarray(g.T), FMT)
    g_bias = bf(np.random.standard_normal(D_OUT) * 0.3)
    return {"x": x,
            "W_words": W_words,
            "W_scales": W_scales,
            "b": b,
            "g_words": g_words,
            "g_scales": g_scales,
            "g_bias": g_bias}


def reference(x, W_words, W_scales, b, g_words, g_scales, g_bias):
    h = (mxq(f64(x), 1, "e4m3") @ unpack_weight(W_words, W_scales, FMT)) + f64(b)
    c = np.cos((mxq(h, 1, "e4m3") @ unpack_weight(g_words, g_scales, FMT)) + f64(g_bias))
    return np.where(np.abs(c) < EPS, -c, c)

@@ -1,0 +1,221 @@
+import math
+from contextlib import ExitStack
+
+import concourse.mybir as mybir
+from concourse.masks import make_identity
+
+F32 = mybir.dt.float32
+BF16 = mybir.dt.bfloat16
+I32 = mybir.dt.int32
+U32 = mybir.dt.uint32
+U8 = mybir.dt.uint8
+FP8X4 = mybir.dt.float8_e4m3fn_x4
+ALU = mybir.AluOpType
+ACT = mybir.ActivationFunctionType
+
+P = 128
+D_IN = 16384
+D_OUT = 1024
+K_PASS = 512
+X_GROUPS = D_IN // K_PASS
+H_GROUPS = D_OUT // K_PASS
+N_TILE = 512
+N_TILES = D_OUT // N_TILE
+WORDS = K_PASS // 2
+PLANES = 4
+
+X_CHUNK_GROUPS = 8
+W_BUFS = 16
+PIECE = 256
+
+EPS = 0.01
+TWO_PI = 2.0 * math.pi
+ROUND = 12582912.0
+
+FLOPS = 2 * P * D_IN * D_OUT + 2 * P * D_OUT * D_OUT
+
+
+def transpose_and_quantise(nc, psum, stage, ident, src_words, groups, codes, planes):
+    flipped = psum.tile([P, groups * 2, P], F32, tag="bank")
+    for i in range(groups):
+        for u in range(2):
+            nc.tensor.transpose(
+                flipped[:, 2 * i + u, :],
+                src_words[:, WORDS * i + u : WORDS * (i + 1) : 2],
+                ident[:],
+            )
+    grouped = stage.tile([P, groups * K_PASS], BF16, tag="grouped", align_bytes=64)
+    nc.scalar.copy(
+        out=grouped[:].bitcast(F32).rearrange("p (i r u) -> p i r u", i=groups, u=2),
+        in_=flipped[:].rearrange("p (i u) r -> p i r u", u=2),
+    )
+    nc.vector.quantize_mx(out=codes.bitcast(FP8X4), scales=planes, in_=grouped[:])
+
+
+def tile_onehiddenlayer_k_kernel(tc, x, W_words, W_scales, b, g_words, g_scales, g_bias, out):
+    nc = tc.nc
+    with ExitStack() as stack:
+        stack.enter_context(tc.manual_schedule())
+        keep = stack.enter_context(tc.tile_pool(name="keep", bufs=1))
+        stage = stack.enter_context(tc.tile_pool(name="stage", bufs=3))
+        w_pool = stack.enter_context(tc.tile_pool(name="w_pool", bufs=W_BUFS))
+        banks = stack.enter_context(tc.psum_pool(name="banks", bufs=4))
+        sums = stack.enter_context(tc.psum_pool(name="sums", bufs=1))
+
+        bias_rows = keep.tile([P, 2 * D_OUT], BF16)
+        nc.vector.memset(bias_rows[:], 0.0)
+        ones = keep.tile([P, P], BF16)
+        nc.vector.memset(ones[:], 1.0)
+        zero = keep.tile([P, 1], F32)
+        nc.vector.memset(zero[:], 0.0)
+        w_planes = keep.tile([P, X_GROUPS // PLANES, D_OUT], U8, align_bytes=64)
+        nc.vector.memset(w_planes[:].bitcast(I32), 0)
+        g_planes = keep.tile([P, D_OUT], U8, align_bytes=64)
+        nc.vector.memset(g_planes[:].bitcast(I32), 0)
+        ident = keep.tile([P, P], F32)
+        make_identity(nc, ident[:])
+        warm = keep.tile([P, 1], F32)
+        nc.scalar.activation(out=warm[:], in_=zero[:], func=ACT.Sin)
+
+        nc.scalar.dma_start(out=bias_rows[0:1, 0:D_OUT], in_=b.rearrange("(o n) -> o n", o=1))
+        nc.scalar.dma_start(out=bias_rows[0:1, D_OUT : 2 * D_OUT], in_=g_bias.rearrange("(o n) -> o n", o=1))
+
+        x_cols = X_CHUNK_GROUPS * K_PASS
+        x_chunks = []
+        for c in range(X_GROUPS // X_CHUNK_GROUPS):
+            x_sb = keep.tile([P, x_cols], BF16, name="x_sb%d" % c)
+            nc.sync.dma_start(out=x_sb[:], in_=x[:, c * x_cols : (c + 1) * x_cols])
+            x_chunks.append(x_sb)
+
+        b_all = keep.tile([P, D_OUT], F32)
+        gb_turns = keep.tile([P, D_OUT], F32)
+        for n in range(N_TILES):
+            cols = slice(n * N_TILE, (n + 1) * N_TILE)
+            spread_b = banks.tile([P, N_TILE], F32, tag="bank")
+            nc.tensor.matmul(spread_b[:], lhsT=ones[:], rhs=bias_rows[:, cols], start=True, stop=True)
+            nc.vector.tensor_copy(out=b_all[:, cols], in_=spread_b[:])
+        for n in range(N_TILES):
+            cols = slice(n * N_TILE, (n + 1) * N_TILE)
+            spread_g = banks.tile([P, N_TILE], F32, tag="bank")
+            nc.tensor.matmul(
+                spread_g[:], lhsT=ones[:], rhs=bias_rows[:, D_OUT + n * N_TILE : D_OUT + (n + 1) * N_TILE],
+                start=True, stop=True,
+            )
+            nc.vector.tensor_scalar(
+                out=gb_turns[:, cols], in0=spread_g[:], scalar1=1.0 / TWO_PI, scalar2=0.25,
+                op0=ALU.mult, op1=ALU.add,
+            )
+
+        x_codes = keep.tile([P, X_GROUPS * P], U32, align_bytes=64)
+        x_planes = keep.tile([P, X_GROUPS * P], U8, align_bytes=64)
+        for c, x_sb in enumerate(x_chunks):
+            x_words = x_sb[:].bitcast(F32)
+            for pair in range(X_CHUNK_GROUPS // 2):
+                first = c * X_CHUNK_GROUPS + 2 * pair
+                transpose_and_quantise(
+                    nc, banks, stage, ident,
+                    x_words[:, 2 * pair * WORDS : 2 * (pair + 1) * WORDS], 2,
+                    x_codes[:, first * P : (first + 2) * P], x_planes[:, first * P : (first + 2) * P],
+                )
+
+        for a in range(X_GROUPS // PLANES):
+            for q in range(4):
+                nc.sync.dma_start(
+                    out=w_planes[32 * q : 32 * q + 4 * PLANES, a, :].bitcast(I32),
+                    in_=W_scales[PLANES * a : PLANES * (a + 1), 4 * q : 4 * q + 4, :].bitcast(I32),
+                )
+        for q in range(4):
+            nc.sync.dma_start(
+                out=g_planes[32 * q : 32 * q + 4 * H_GROUPS, :].bitcast(I32),
+                in_=g_scales[:, 4 * q : 4 * q + 4, :].bitcast(I32),
+            )
+
+        h_sums = [sums.tile([P, N_TILE], F32, name="h_sum%d" % n) for n in range(N_TILES)]
+        for g in range(X_GROUPS):
+            w_sb = w_pool.tile([P, D_OUT], U32, tag="w_sb", align_bytes=64)
+            nc.sync.dma_start(
+                out=w_sb[:].bitcast(I32), in_=W_words[g].rearrange("p n t -> p (n t)").bitcast(I32)
+            )
+            a, j = divmod(g, PLANES)
+            for n in range(N_TILES):
+                cols = slice(n * N_TILE, (n + 1) * N_TILE)
+                nc.tensor.matmul_mx(
+                    out=h_sums[n][:],
+                    lhsT=x_codes[:, g * P : (g + 1) * P].bitcast(FP8X4),
+                    lhsT_scale=x_planes[:, g * P : (g + 1) * P],
+                    rhs=w_sb[:, cols].bitcast(FP8X4),
+                    rhs_scale=w_planes[4 * j : P, a, cols],
+                    start=(g == 0),
+                    stop=(g == X_GROUPS - 1),
+                )
+
+        g_sb = []
+        for k in range(H_GROUPS):
+            g_tile = keep.tile([P, D_OUT], U32, name="g_sb%d" % k, align_bytes=64)
+            nc.sync.dma_start(
+                out=g_tile[:].bitcast(I32), in_=g_words[k].rearrange("p n t -> p (n t)").bitcast(I32)
+            )
+            g_sb.append(g_tile)
+
+        h_bf = []
+        for k in range(H_GROUPS):
+            h_tile = keep.tile([P, K_PASS], BF16, name="h_bf%d" % k)
+            nc.vector.tensor_tensor(
+                out=h_tile[:], in0=h_sums[k][:], in1=b_all[:, k * K_PASS : (k + 1) * K_PASS], op=ALU.add
+            )
+            h_bf.append(h_tile)
+        h_codes = keep.tile([P, H_GROUPS * P], U32, align_bytes=64)
+        h_planes = keep.tile([P, H_GROUPS * P], U8, align_bytes=64)
+        for k in range(H_GROUPS):
+            transpose_and_quantise(
+                nc, banks, stage, ident, h_bf[k][:].bitcast(F32), 1,
+                h_codes[:, k * P : (k + 1) * P], h_planes[:, k * P : (k + 1) * P],
+            )
+
+        z_sums = [sums.tile([P, N_TILE], F32, name="z_sum%d" % n) for n in range(N_TILES)]
+        for k in range(H_GROUPS):
+            for n in range(N_TILES):
+                cols = slice(n * N_TILE, (n + 1) * N_TILE)
+                nc.tensor.matmul_mx(
+                    out=z_sums[n][:],
+                    lhsT=h_codes[:, k * P : (k + 1) * P].bitcast(FP8X4),
+                    lhsT_scale=h_planes[:, k * P : (k + 1) * P],
+                    rhs=g_sb[k][:, cols].bitcast(FP8X4),
+                    rhs_scale=g_planes[4 * k : P, cols],
+                    start=(k == 0),
+                    stop=(k == H_GROUPS - 1),
+                )
+
+        turns = keep.tile([P, D_OUT], F32)
+        shifted = keep.tile([P, D_OUT], F32)
+        neg_frac = keep.tile([P, D_OUT], F32)
+        cosine = keep.tile([P, D_OUT], F32)
+        size = keep.tile([P, D_OUT], F32)
+        keep2 = keep.tile([P, D_OUT], F32)
+        result = keep.tile([P, D_OUT], F32)
+        pieces = [slice(i * PIECE, (i + 1) * PIECE) for i in range(D_OUT // PIECE)]
+        for i, cols in enumerate(pieces):
+            n, first = divmod(i * PIECE, N_TILE)
+            nc.vector.scalar_tensor_tensor(
+                out=turns[:, cols], in0=z_sums[n][:, first : first + PIECE], scalar=1.0 / TWO_PI,
+                in1=gb_turns[:, cols], op0=ALU.mult, op1=ALU.add,
+            )
+        for cols in pieces:
+            nc.scalar.activation(out=shifted[:, cols], in_=turns[:, cols], func=ACT.Identity, bias=ROUND)
+        for cols in pieces:
+            nc.vector.scalar_tensor_tensor(
+                out=neg_frac[:, cols], in0=shifted[:, cols], scalar=ROUND, in1=turns[:, cols],
+                op0=ALU.subtract, op1=ALU.subtract,
+            )
+        for cols in pieces:
+            nc.scalar.activation(out=cosine[:, cols], in_=neg_frac[:, cols], func=ACT.Sin, scale=-TWO_PI)
+            nc.scalar.activation(out=size[:, cols], in_=cosine[:, cols], func=ACT.Abs)
+        for cols in pieces:
+            nc.vector.tensor_scalar(
+                out=keep2[:, cols], in0=size[:, cols], scalar1=EPS, scalar2=2.0, op0=ALU.is_gt, op1=ALU.mult
+            )
+            nc.vector.scalar_tensor_tensor(
+                out=result[:, cols], in0=keep2[:, cols], scalar=1.0, in1=cosine[:, cols],
+                op0=ALU.subtract, op1=ALU.mult,
+            )
+            nc.sync.dma_start(out=out[:, cols], in_=result[:, cols])

@@ -124,11 +124,6 @@ def tile_onehiddenlayer_k_kernel(tc, x, W_words, W_scales, b, g_words, g_scales,
                     out=w_planes[32 * q : 32 * q + 4 * PLANES, a, :].bitcast(I32),
                     in_=W_scales[PLANES * a : PLANES * (a + 1), 4 * q : 4 * q + 4, :].bitcast(I32),
                 )
-        for q in range(4):
-            nc.sync.dma_start(
-                out=g_planes[32 * q : 32 * q + 4 * H_GROUPS, :].bitcast(I32),
-                in_=g_scales[:, 4 * q : 4 * q + 4, :].bitcast(I32),
-            )
 
         h_sums = [sums.tile([P, N_TILE], F32, name="h_sum%d" % n) for n in range(N_TILES)]
         for g in range(X_GROUPS):
@@ -149,6 +144,11 @@ def tile_onehiddenlayer_k_kernel(tc, x, W_words, W_scales, b, g_words, g_scales,
                     stop=(g == X_GROUPS - 1),
                 )
 
+        for q in range(4):
+            nc.sync.dma_start(
+                out=g_planes[32 * q : 32 * q + 4 * H_GROUPS, :].bitcast(I32),
+                in_=g_scales[:, 4 * q : 4 * q + 4, :].bitcast(I32),
+            )
         g_sb = []
         for k in range(H_GROUPS):
             g_tile = keep.tile([P, D_OUT], U32, name="g_sb%d" % k, align_bytes=64)

import math
from contextlib import ExitStack

import concourse.mybir as mybir
from concourse.masks import make_identity

F32 = mybir.dt.float32
BF16 = mybir.dt.bfloat16
I32 = mybir.dt.int32
U32 = mybir.dt.uint32
U8 = mybir.dt.uint8
FP8X4 = mybir.dt.float8_e4m3fn_x4
ALU = mybir.AluOpType
ACT = mybir.ActivationFunctionType

P = 128
D_IN = 16384
D_OUT = 1024
K_PASS = 512
X_GROUPS = D_IN // K_PASS
H_GROUPS = D_OUT // K_PASS
N_TILE = 512
N_TILES = D_OUT // N_TILE
WORDS = K_PASS // 2
PLANES = 4

X_CHUNK_GROUPS = 8
W_BUFS = 16
PIECE = 256

EPS = 0.01
TWO_PI = 2.0 * math.pi
ROUND = 12582912.0

FLOPS = 2 * P * D_IN * D_OUT + 2 * P * D_OUT * D_OUT


def transpose_and_quantise(nc, psum, stage, ident, src_words, groups, codes, planes):
    flipped = psum.tile([P, groups * 2, P], F32, tag="bank")
    for i in range(groups):
        for u in range(2):
            nc.tensor.transpose(
                flipped[:, 2 * i + u, :],
                src_words[:, WORDS * i + u : WORDS * (i + 1) : 2],
                ident[:],
            )
    grouped = stage.tile([P, groups * K_PASS], BF16, tag="grouped", align_bytes=64)
    nc.scalar.copy(
        out=grouped[:].bitcast(F32).rearrange("p (i r u) -> p i r u", i=groups, u=2),
        in_=flipped[:].rearrange("p (i u) r -> p i r u", u=2),
    )
    nc.vector.quantize_mx(out=codes.bitcast(FP8X4), scales=planes, in_=grouped[:])


def tile_onehiddenlayer_k_kernel(tc, x, W_words, W_scales, b, g_words, g_scales, g_bias, out):
    nc = tc.nc
    with ExitStack() as stack:
        stack.enter_context(tc.manual_schedule())
        keep = stack.enter_context(tc.tile_pool(name="keep", bufs=1))
        stage = stack.enter_context(tc.tile_pool(name="stage", bufs=3))
        w_pool = stack.enter_context(tc.tile_pool(name="w_pool", bufs=W_BUFS))
        banks = stack.enter_context(tc.psum_pool(name="banks", bufs=4))
        sums = stack.enter_context(tc.psum_pool(name="sums", bufs=1))

        bias_rows = keep.tile([P, 2 * D_OUT], BF16)
        nc.vector.memset(bias_rows[:], 0.0)
        ones = keep.tile([P, P], BF16)
        nc.vector.memset(ones[:], 1.0)
        zero = keep.tile([P, 1], F32)
        nc.vector.memset(zero[:], 0.0)
        w_planes = keep.tile([P, X_GROUPS // PLANES, D_OUT], U8, align_bytes=64)
        nc.vector.memset(w_planes[:].bitcast(I32), 0)
        g_planes = keep.tile([P, D_OUT], U8, align_bytes=64)
        nc.vector.memset(g_planes[:].bitcast(I32), 0)
        ident = keep.tile([P, P], F32)
        make_identity(nc, ident[:])
        warm = keep.tile([P, 1], F32)
        nc.scalar.activation(out=warm[:], in_=zero[:], func=ACT.Sin)

        nc.scalar.dma_start(out=bias_rows[0:1, 0:D_OUT], in_=b.rearrange("(o n) -> o n", o=1))
        nc.scalar.dma_start(out=bias_rows[0:1, D_OUT : 2 * D_OUT], in_=g_bias.rearrange("(o n) -> o n", o=1))

        x_cols = X_CHUNK_GROUPS * K_PASS
        x_chunks = []
        for c in range(X_GROUPS // X_CHUNK_GROUPS):
            x_sb = keep.tile([P, x_cols], BF16, name="x_sb%d" % c)
            nc.sync.dma_start(out=x_sb[:], in_=x[:, c * x_cols : (c + 1) * x_cols])
            x_chunks.append(x_sb)

        b_all = keep.tile([P, D_OUT], F32)
        gb_turns = keep.tile([P, D_OUT], F32)
        for n in range(N_TILES):
            cols = slice(n * N_TILE, (n + 1) * N_TILE)
            spread_b = banks.tile([P, N_TILE], F32, tag="bank")
            nc.tensor.matmul(spread_b[:], lhsT=ones[:], rhs=bias_rows[:, cols], start=True, stop=True)
            nc.vector.tensor_copy(out=b_all[:, cols], in_=spread_b[:])
        for n in range(N_TILES):
            cols = slice(n * N_TILE, (n + 1) * N_TILE)
            spread_g = banks.tile([P, N_TILE], F32, tag="bank")
            nc.tensor.matmul(
                spread_g[:], lhsT=ones[:], rhs=bias_rows[:, D_OUT + n * N_TILE : D_OUT + (n + 1) * N_TILE],
                start=True, stop=True,
            )
            nc.vector.tensor_scalar(
                out=gb_turns[:, cols], in0=spread_g[:], scalar1=1.0 / TWO_PI, scalar2=0.25,
                op0=ALU.mult, op1=ALU.add,
            )

        x_codes = keep.tile([P, X_GROUPS * P], U32, align_bytes=64)
        x_planes = keep.tile([P, X_GROUPS * P], U8, align_bytes=64)
        for c, x_sb in enumerate(x_chunks):
            x_words = x_sb[:].bitcast(F32)
            for pair in range(X_CHUNK_GROUPS // 2):
                first = c * X_CHUNK_GROUPS + 2 * pair
                transpose_and_quantise(
                    nc, banks, stage, ident,
                    x_words[:, 2 * pair * WORDS : 2 * (pair + 1) * WORDS], 2,
                    x_codes[:, first * P : (first + 2) * P], x_planes[:, first * P : (first + 2) * P],
                )

        for a in range(X_GROUPS // PLANES):
            for q in range(4):
                nc.sync.dma_start(
                    out=w_planes[32 * q : 32 * q + 4 * PLANES, a, :].bitcast(I32),
                    in_=W_scales[PLANES * a : PLANES * (a + 1), 4 * q : 4 * q + 4, :].bitcast(I32),
                )

        h_sums = [sums.tile([P, N_TILE], F32, name="h_sum%d" % n) for n in range(N_TILES)]
        for g in range(X_GROUPS):
            w_sb = w_pool.tile([P, D_OUT], U32, tag="w_sb", align_bytes=64)
            nc.sync.dma_start(
                out=w_sb[:].bitcast(I32), in_=W_words[g].rearrange("p n t -> p (n t)").bitcast(I32)
            )
            a, j = divmod(g, PLANES)
            for n in range(N_TILES):
                cols = slice(n * N_TILE, (n + 1) * N_TILE)
                nc.tensor.matmul_mx(
                    out=h_sums[n][:],
                    lhsT=x_codes[:, g * P : (g + 1) * P].bitcast(FP8X4),
                    lhsT_scale=x_planes[:, g * P : (g + 1) * P],
                    rhs=w_sb[:, cols].bitcast(FP8X4),
                    rhs_scale=w_planes[4 * j : P, a, cols],
                    start=(g == 0),
                    stop=(g == X_GROUPS - 1),
                )

        for q in range(4):
            nc.sync.dma_start(
                out=g_planes[32 * q : 32 * q + 4 * H_GROUPS, :].bitcast(I32),
                in_=g_scales[:, 4 * q : 4 * q + 4, :].bitcast(I32),
            )
        g_sb = []
        for k in range(H_GROUPS):
            g_tile = keep.tile([P, D_OUT], U32, name="g_sb%d" % k, align_bytes=64)
            nc.sync.dma_start(
                out=g_tile[:].bitcast(I32), in_=g_words[k].rearrange("p n t -> p (n t)").bitcast(I32)
            )
            g_sb.append(g_tile)

        h_bf = []
        for k in range(H_GROUPS):
            h_tile = keep.tile([P, K_PASS], BF16, name="h_bf%d" % k)
            nc.vector.tensor_tensor(
                out=h_tile[:], in0=h_sums[k][:], in1=b_all[:, k * K_PASS : (k + 1) * K_PASS], op=ALU.add
            )
            h_bf.append(h_tile)
        h_codes = keep.tile([P, H_GROUPS * P], U32, align_bytes=64)
        h_planes = keep.tile([P, H_GROUPS * P], U8, align_bytes=64)
        for k in range(H_GROUPS):
            transpose_and_quantise(
                nc, banks, stage, ident, h_bf[k][:].bitcast(F32), 1,
                h_codes[:, k * P : (k + 1) * P], h_planes[:, k * P : (k + 1) * P],
            )

        z_sums = [sums.tile([P, N_TILE], F32, name="z_sum%d" % n) for n in range(N_TILES)]
        for k in range(H_GROUPS):
            for n in range(N_TILES):
                cols = slice(n * N_TILE, (n + 1) * N_TILE)
                nc.tensor.matmul_mx(
                    out=z_sums[n][:],
                    lhsT=h_codes[:, k * P : (k + 1) * P].bitcast(FP8X4),
                    lhsT_scale=h_planes[:, k * P : (k + 1) * P],
                    rhs=g_sb[k][:, cols].bitcast(FP8X4),
                    rhs_scale=g_planes[4 * k : P, cols],
                    start=(k == 0),
                    stop=(k == H_GROUPS - 1),
                )

        turns = keep.tile([P, D_OUT], F32)
        shifted = keep.tile([P, D_OUT], F32)
        neg_frac = keep.tile([P, D_OUT], F32)
        cosine = keep.tile([P, D_OUT], F32)
        size = keep.tile([P, D_OUT], F32)
        keep2 = keep.tile([P, D_OUT], F32)
        result = keep.tile([P, D_OUT], F32)
        pieces = [slice(i * PIECE, (i + 1) * PIECE) for i in range(D_OUT // PIECE)]
        for i, cols in enumerate(pieces):
            n, first = divmod(i * PIECE, N_TILE)
            nc.vector.scalar_tensor_tensor(
                out=turns[:, cols], in0=z_sums[n][:, first : first + PIECE], scalar=1.0 / TWO_PI,
                in1=gb_turns[:, cols], op0=ALU.mult, op1=ALU.add,
            )
        for cols in pieces:
            nc.scalar.activation(out=shifted[:, cols], in_=turns[:, cols], func=ACT.Identity, bias=ROUND)
        for cols in pieces:
            nc.vector.scalar_tensor_tensor(
                out=neg_frac[:, cols], in0=shifted[:, cols], scalar=ROUND, in1=turns[:, cols],
                op0=ALU.subtract, op1=ALU.subtract,
            )
        for cols in pieces:
            nc.scalar.activation(out=cosine[:, cols], in_=neg_frac[:, cols], func=ACT.Sin, scale=-TWO_PI)
            nc.scalar.activation(out=size[:, cols], in_=cosine[:, cols], func=ACT.Abs)
        for cols in pieces:
            nc.vector.tensor_scalar(
                out=keep2[:, cols], in0=size[:, cols], scalar1=EPS, scalar2=2.0, op0=ALU.is_gt, op1=ALU.mult
            )
            nc.vector.scalar_tensor_tensor(
                out=result[:, cols], in0=keep2[:, cols], scalar=1.0, in1=cosine[:, cols],
                op0=ALU.subtract, op1=ALU.mult,
            )
            nc.sync.dma_start(out=out[:, cols], in_=result[:, cols])
